import numpy as np
import ml_dtypes

BF16 = ml_dtypes.bfloat16


def bf(x):
    return np.asarray(x, np.float32).astype(BF16)


def f32(x):
    return np.asarray(x, np.float32)


def f64(x):
    return np.asarray(x).astype(np.float64)


def striped(idx):
    return np.tile(idx.reshape(-1, 16).T, (8, 1))


F, D1, E, H, Q, S, K, HALF, N = 1024, 512, 256, 256, 128, 2048, 2, 1024, 4096
BN_EPS = 1e-5


def col(rows, centre):
    return f32(centre + 0.1 * np.random.standard_normal((rows, 1)))


def var_col(rows):
    return f32(0.5 + np.random.random_sample((rows, 1)))


def bn_relu(z, b, gain, shift, mean, var):
    return np.maximum((z + f64(b) - f64(mean)) * (f64(gain) / np.sqrt(f64(var) + BN_EPS)) + f64(shift), 0.0)


def setup_inputs():
    return {
        "feature": f32(np.random.standard_normal((F, S))),
        "enc_w1": bf(np.random.standard_normal((F, D1)) / np.sqrt(F)),
        "enc_b1": col(D1, 0.0),
        "bn1_gain": col(D1, 1.0),
        "bn1_shift": col(D1, 0.0),
        "bn1_mean": col(D1, 0.0),
        "bn1_var": var_col(D1),
        "enc_w2": bf(np.random.standard_normal((D1, E)) * np.sqrt(2.0 / D1)),
        "enc_b2": col(E, 0.0),
        "bn2_gain": col(E, 1.0),
        "bn2_shift": col(E, 0.0),
        "bn2_mean": col(E, 0.0),
        "bn2_var": var_col(E),
        "gcn1_w": bf(np.random.standard_normal((E, H)) * np.sqrt(2.0 / E)),
        "gcn1_b": col(H, 0.0),
        "gcn2_w": bf(np.random.standard_normal((H, Q)) * np.sqrt(2.0 / H)),
        "offs": striped(np.concatenate([np.random.permutation(S)[:HALF] for _ in range(N // HALF)])),
    }


def reference(feature, enc_w1, enc_b1, bn1_gain, bn1_shift, bn1_mean, bn1_var, enc_w2, enc_b2, bn2_gain, bn2_shift, bn2_mean, bn2_var, gcn1_w, gcn1_b, gcn2_w, offs):
    idx = offs[:16].T.reshape(-1)
    a1 = bn_relu(f64(enc_w1).T @ f64(feature), enc_b1, bn1_gain, bn1_shift, bn1_mean, bn1_var)
    a2 = bn_relu(f64(enc_w2).T @ a1, enc_b2, bn2_gain, bn2_shift, bn2_mean, bn2_var)
    xw = f64(gcn1_w).T @ a2
    acc = xw.copy()
    for r in range(K):
        acc = xw[:, idx[r * S:(r + 1) * S]] + acc
    a3 = np.maximum(acc / (K + 1) + f64(gcn1_b), 0.0)
    return f64(gcn2_w).T @ a3

@@ -1,0 +1,189 @@
+import concourse.mybir as mybir
+
+F32 = mybir.dt.float32
+BF16 = mybir.dt.bfloat16
+U16 = mybir.dt.uint16
+ADD = mybir.AluOpType.add
+SUBTRACT = mybir.AluOpType.subtract
+MULT = mybir.AluOpType.mult
+POW = mybir.AluOpType.pow
+RELU = mybir.ActivationFunctionType.Relu
+
+P = 128
+F, D1, E, H, Q = 1024, 512, 256, 256, 128
+S = 2048
+ROUNDS = 2
+BN_EPS = 1e-5
+BANK = 512
+PIECE = 1024
+
+FLOPS = 2 * S * (F * D1 + D1 * E + E * H + H * Q)
+
+
+def rows_in_blocks(matrix, blocks):
+    return matrix.rearrange("(p c) n -> p c n", c=blocks)
+
+
+def columns_of_block(weights, blocks, c):
+    return weights.rearrange("p (j c) -> p c j", c=blocks)[:, c, :]
+
+
+def load_column(nc, pool, column, name):
+    blocks = column.shape[0] // P
+    tile = pool.tile([P, blocks], F32, name=name)
+    nc.gpsimd.dma_start(tile[:], column.rearrange("(p c) one -> p (c one)", c=blocks))
+    return tile
+
+
+def fold_batch_norm(nc, pool, layer, lin_bias, gain, shift, mean, var, minus_half):
+    blocks = var.shape[1]
+    scale = pool.tile([P, blocks], F32, name=f"scale{layer}")
+    bias = pool.tile([P, blocks], F32, name=f"bias{layer}")
+    nc.gpsimd.tensor_scalar(out=scale[:], in0=var[:], scalar1=BN_EPS, scalar2=None, op0=ADD)
+    nc.gpsimd.tensor_tensor(out=scale[:], in0=scale[:], in1=minus_half[:, 0:blocks], op=POW)
+    nc.gpsimd.tensor_tensor(out=scale[:], in0=scale[:], in1=gain[:], op=MULT)
+    nc.gpsimd.tensor_tensor(out=bias[:], in0=lin_bias[:], in1=mean[:], op=SUBTRACT)
+    nc.gpsimd.tensor_tensor(out=bias[:], in0=bias[:], in1=scale[:], op=MULT)
+    nc.gpsimd.tensor_tensor(out=bias[:], in0=bias[:], in1=shift[:], op=ADD)
+    return scale, bias
+
+
+def tile_gcnclassifer_b_kernel(
+    tc,
+    feature,
+    enc_w1,
+    enc_b1,
+    bn1_gain,
+    bn1_shift,
+    bn1_mean,
+    bn1_var,
+    enc_w2,
+    enc_b2,
+    bn2_gain,
+    bn2_shift,
+    bn2_mean,
+    bn2_var,
+    gcn1_w,
+    gcn1_b,
+    gcn2_w,
+    offs,
+    out,
+):
+    nc = tc.nc
+    f_blocks, d_blocks, e_blocks, h_blocks = F // P, D1 // P, E // P, H // P
+    banks = S // BANK
+
+    with (
+        tc.tile_pool(name="held", bufs=1) as held,
+        tc.tile_pool(name="staged", bufs=8) as staged,
+        tc.tile_pool(name="rounded", bufs=16) as rounded,
+        tc.tile_pool(name="results", bufs=2) as results,
+        tc.psum_pool(name="psum", bufs=8) as psum,
+    ):
+        lin_b1 = load_column(nc, held, enc_b1, "lin_b1")
+        gain1 = load_column(nc, held, bn1_gain, "gain1")
+        shift1 = load_column(nc, held, bn1_shift, "shift1")
+        mean1 = load_column(nc, held, bn1_mean, "mean1")
+        var1 = load_column(nc, held, bn1_var, "var1")
+        lin_b2 = load_column(nc, held, enc_b2, "lin_b2")
+        gain2 = load_column(nc, held, bn2_gain, "gain2")
+        shift2 = load_column(nc, held, bn2_shift, "shift2")
+        mean2 = load_column(nc, held, bn2_mean, "mean2")
+        var2 = load_column(nc, held, bn2_var, "var2")
+        bias3 = load_column(nc, held, gcn1_b, "bias3")
+        minus_half = held.tile([P, d_blocks], F32, name="minus_half")
+        nc.gpsimd.memset(minus_half[:], -0.5)
+        scale1, bias1 = fold_batch_norm(nc, held, 1, lin_b1, gain1, shift1, mean1, var1, minus_half)
+        scale2, bias2 = fold_batch_norm(nc, held, 2, lin_b2, gain2, shift2, mean2, var2, minus_half)
+
+        w1 = [held.tile([P, D1], BF16, name=f"w1_{k}") for k in range(f_blocks)]
+        for k in range(f_blocks):
+            nc.scalar.dma_start(w1[k][:], rows_in_blocks(enc_w1, f_blocks)[:, k, :])
+        w2 = held.tile([P, d_blocks, E], BF16, name="w2")
+        nc.scalar.dma_start(w2[:], rows_in_blocks(enc_w2, d_blocks))
+        w3 = held.tile([P, e_blocks, H], BF16, name="w3")
+        nc.scalar.dma_start(w3[:], rows_in_blocks(gcn1_w, e_blocks))
+        w4 = held.tile([P, h_blocks, Q], BF16, name="w4")
+        nc.scalar.dma_start(w4[:], rows_in_blocks(gcn2_w, h_blocks))
+
+        a1 = [[held.tile([P, BANK], BF16, name=f"a1_{m}_{n}") for n in range(banks)] for m in range(d_blocks)]
+        for n in range(banks):
+            z1 = [psum.tile([P, BANK], F32, name=f"z1_{m}", tag="bank") for m in range(d_blocks)]
+            for k in range(f_blocks):
+                loaded = staged.tile([P, BANK], F32, name="loaded")
+                nc.sync.dma_start(loaded[:], rows_in_blocks(feature, f_blocks)[:, k, n * BANK : (n + 1) * BANK])
+                x = rounded.tile([P, BANK], BF16, name="x")
+                nc.vector.tensor_copy(x[:], loaded[:])
+                for m in range(d_blocks):
+                    nc.tensor.matmul(
+                        z1[m][:],
+                        columns_of_block(w1[k][:], d_blocks, m),
+                        x[:],
+                        start=(k == 0),
+                        stop=(k == f_blocks - 1),
+                    )
+            for m in range(d_blocks):
+                nc.scalar.activation(
+                    a1[m][n][:], z1[m][:], RELU, bias=bias1[:, m : m + 1], scale=scale1[:, m : m + 1]
+                )
+
+        offsets = held.tile([P, ROUNDS * S // 16], U16, name="offsets")
+        nc.sync.dma_start(offsets[:], offs)
+
+        a2 = [[held.tile([P, BANK], BF16, name=f"a2_{m}_{n}") for n in range(banks)] for m in range(e_blocks)]
+        for n in range(banks):
+            for m in range(e_blocks):
+                z2 = psum.tile([P, BANK], F32, name="z2", tag="bank")
+                for k in range(d_blocks):
+                    nc.tensor.matmul(
+                        z2[:],
+                        columns_of_block(w2[:, k, :], e_blocks, m),
+                        a1[k][n][:],
+                        start=(k == 0),
+                        stop=(k == d_blocks - 1),
+                    )
+                nc.scalar.activation(a2[m][n][:], z2[:], RELU, bias=bias2[:, m : m + 1], scale=scale2[:, m : m + 1])
+
+        xw = [held.tile([P, S], F32, name=f"xw_{h}") for h in range(h_blocks)]
+        sums = [[held.tile([P, S], F32, name=f"sum_{h}_{i}") for i in range(2)] for h in range(h_blocks)]
+        for h in range(h_blocks):
+            for n in range(banks):
+                product = psum.tile([P, BANK], F32, name="product", tag="bank")
+                for k in range(e_blocks):
+                    nc.tensor.matmul(
+                        product[:],
+                        columns_of_block(w3[:, k, :], h_blocks, h),
+                        a2[k][n][:],
+                        start=(k == 0),
+                        stop=(k == e_blocks - 1),
+                    )
+                nc.scalar.copy(xw[h][:, n * BANK : (n + 1) * BANK], product[:])
+                nc.scalar.copy(sums[h][0][:, n * BANK : (n + 1) * BANK], product[:])
+
+        a3 = [[held.tile([P, BANK], BF16, name=f"a3_{h}_{n}") for n in range(banks)] for h in range(h_blocks)]
+        for g in range(S // PIECE):
+            nodes = slice(g * PIECE, (g + 1) * PIECE)
+            for h in range(h_blocks):
+                for r in range(ROUNDS):
+                    first = (r * S + g * PIECE) // 16
+                    nc.vector.tensor_tensor(
+                        out=sums[h][(r + 1) % 2][:, nodes],
+                        in0=xw[h][:].indirect(offsets[:, first : first + PIECE // 16]),
+                        in1=sums[h][r % 2][:, nodes],
+                        op=ADD,
+                    )
+                for n in range(g * PIECE // BANK, (g + 1) * PIECE // BANK):
+                    nc.scalar.activation(
+                        a3[h][n][:],
+                        sums[h][ROUNDS % 2][:, n * BANK : (n + 1) * BANK],
+                        RELU,
+                        bias=bias3[:, h : h + 1],
+                        scale=1.0 / (ROUNDS + 1),
+                    )
+            for n in range(g * PIECE // BANK, (g + 1) * PIECE // BANK):
+                y = psum.tile([P, BANK], F32, name="y", tag="bank")
+                for h in range(h_blocks):
+                    nc.tensor.matmul(y[:], w4[:, h, :], a3[h][n][:], start=(h == 0), stop=(h == h_blocks - 1))
+                result = results.tile([P, BANK], F32, name="result")
+                nc.scalar.copy(result[:], y[:])
+                nc.sync.dma_start(out[:, n * BANK : (n + 1) * BANK], result[:])

@@ -15,7 +15,9 @@ S = 2048
 ROUNDS = 2
 BN_EPS = 1e-5
 BANK = 512
-PIECE = 1024
+WARM_UP = 5
+PIECES = (1024, 512, 256, 256)
+assert sum(PIECES) == S
 
 FLOPS = 2 * S * (F * D1 + D1 * E + E * H + H * Q)
 
@@ -80,6 +82,12 @@ def tile_gcnclassifer_b_kernel(
         tc.tile_pool(name="results", bufs=2) as results,
         tc.psum_pool(name="psum", bufs=8) as psum,
     ):
+        zeros = held.tile([P, BANK], BF16, name="zeros")
+        nc.vector.memset(zeros[:], 0.0)
+        unread = psum.tile([P, BANK], F32, name="unread", tag="bank")
+        for i in range(WARM_UP):
+            nc.tensor.matmul(unread[:], zeros[:, 0:P], zeros[:], start=True, stop=True)
+
         lin_b1 = load_column(nc, held, enc_b1, "lin_b1")
         gain1 = load_column(nc, held, bn1_gain, "gain1")
         shift1 = load_column(nc, held, bn1_shift, "shift1")
@@ -158,32 +166,39 @@ def tile_gcnclassifer_b_kernel(
                         stop=(k == e_blocks - 1),
                     )
                 nc.scalar.copy(xw[h][:, n * BANK : (n + 1) * BANK], product[:])
-                nc.scalar.copy(sums[h][0][:, n * BANK : (n + 1) * BANK], product[:])
+                if h == 0:
+                    nc.vector.tensor_copy(sums[h][0][:, n * BANK : (n + 1) * BANK], xw[h][:, n * BANK : (n + 1) * BANK])
+                else:
+                    nc.scalar.copy(sums[h][0][:, n * BANK : (n + 1) * BANK], product[:])
 
-        a3 = [[held.tile([P, BANK], BF16, name=f"a3_{h}_{n}") for n in range(banks)] for h in range(h_blocks)]
-        for g in range(S // PIECE):
-            nodes = slice(g * PIECE, (g + 1) * PIECE)
+        a3 = [held.tile([P, S], BF16, name=f"a3_{h}") for h in range(h_blocks)]
+        begin = 0
+        for width in PIECES:
+            end = begin + width
+            chunks = [(lo, min(lo + BANK, end)) for lo in range(begin, end, BANK)]
+            y = [psum.tile([P, BANK], F32, name=f"y_{lo}", tag="bank") for lo, hi in chunks]
             for h in range(h_blocks):
                 for r in range(ROUNDS):
-                    first = (r * S + g * PIECE) // 16
+                    first = (r * S + begin) // 16
                     nc.vector.tensor_tensor(
-                        out=sums[h][(r + 1) % 2][:, nodes],
-                        in0=xw[h][:].indirect(offsets[:, first : first + PIECE // 16]),
-                        in1=sums[h][r % 2][:, nodes],
+                        out=sums[h][(r + 1) % 2][:, begin:end],
+                        in0=xw[h][:].indirect(offsets[:, first : first + width // 16]),
+                        in1=sums[h][r % 2][:, begin:end],
                         op=ADD,
                     )
-                for n in range(g * PIECE // BANK, (g + 1) * PIECE // BANK):
+                for (lo, hi), y_chunk in zip(chunks, y):
                     nc.scalar.activation(
-                        a3[h][n][:],
-                        sums[h][ROUNDS % 2][:, n * BANK : (n + 1) * BANK],
+                        a3[h][:, lo:hi],
+                        sums[h][ROUNDS % 2][:, lo:hi],
                         RELU,
                         bias=bias3[:, h : h + 1],
                         scale=1.0 / (ROUNDS + 1),
                     )
-            for n in range(g * PIECE // BANK, (g + 1) * PIECE // BANK):
-                y = psum.tile([P, BANK], F32, name="y", tag="bank")
-                for h in range(h_blocks):
-                    nc.tensor.matmul(y[:], w4[:, h, :], a3[h][n][:], start=(h == 0), stop=(h == h_blocks - 1))
+                    nc.tensor.matmul(
+                        y_chunk[:, 0 : hi - lo], w4[:, h, :], a3[h][:, lo:hi], start=(h == 0), stop=(h == h_blocks - 1)
+                    )
+            for (lo, hi), y_chunk in zip(chunks, y):
                 result = results.tile([P, BANK], F32, name="result")
-                nc.scalar.copy(result[:], y[:])
-                nc.sync.dma_start(out[:, n * BANK : (n + 1) * BANK], result[:])
+                nc.scalar.copy(result[:, 0 : hi - lo], y_chunk[:, 0 : hi - lo])
+                nc.sync.dma_start(out[:, lo:hi], result[:, 0 : hi - lo])
+            begin = end

@@ -15,7 +15,6 @@ S = 2048
 ROUNDS = 2
 BN_EPS = 1e-5
 BANK = 512
-WARM_UP = 5
 PIECES = (1024, 512, 256, 256)
 assert sum(PIECES) == S
 
@@ -82,12 +81,6 @@ def tile_gcnclassifer_b_kernel(
         tc.tile_pool(name="results", bufs=2) as results,
         tc.psum_pool(name="psum", bufs=8) as psum,
     ):
-        zeros = held.tile([P, BANK], BF16, name="zeros")
-        nc.vector.memset(zeros[:], 0.0)
-        unread = psum.tile([P, BANK], F32, name="unread", tag="bank")
-        for i in range(WARM_UP):
-            nc.tensor.matmul(unread[:], zeros[:, 0:P], zeros[:], start=True, stop=True)
-
         lin_b1 = load_column(nc, held, enc_b1, "lin_b1")
         gain1 = load_column(nc, held, bn1_gain, "gain1")
         shift1 = load_column(nc, held, bn1_shift, "shift1")

@@ -15,6 +15,7 @@ S = 2048
 ROUNDS = 2
 BN_EPS = 1e-5
 BANK = 512
+WARM_UP = 5
 PIECES = (1024, 512, 256, 256)
 assert sum(PIECES) == S
 
@@ -78,9 +79,14 @@ def tile_gcnclassifer_b_kernel(
         tc.tile_pool(name="held", bufs=1) as held,
         tc.tile_pool(name="staged", bufs=8) as staged,
         tc.tile_pool(name="rounded", bufs=16) as rounded,
-        tc.tile_pool(name="results", bufs=2) as results,
         tc.psum_pool(name="psum", bufs=8) as psum,
     ):
+        zeros = held.tile([P, BANK], BF16, name="zeros")
+        nc.vector.memset(zeros[:], 0.0)
+        unread = psum.tile([P, BANK], F32, name="unread", tag="bank")
+        for i in range(WARM_UP):
+            nc.tensor.matmul(unread[:], zeros[:, 0:P], zeros[:], start=True, stop=True)
+
         lin_b1 = load_column(nc, held, enc_b1, "lin_b1")
         gain1 = load_column(nc, held, bn1_gain, "gain1")
         shift1 = load_column(nc, held, bn1_shift, "shift1")
@@ -158,13 +164,15 @@ def tile_gcnclassifer_b_kernel(
                         start=(k == 0),
                         stop=(k == e_blocks - 1),
                     )
-                nc.scalar.copy(xw[h][:, n * BANK : (n + 1) * BANK], product[:])
                 if h == 0:
-                    nc.vector.tensor_copy(sums[h][0][:, n * BANK : (n + 1) * BANK], xw[h][:, n * BANK : (n + 1) * BANK])
+                    nc.vector.tensor_copy(xw[h][:, n * BANK : (n + 1) * BANK], product[:])
+                    nc.scalar.copy(sums[h][0][:, n * BANK : (n + 1) * BANK], xw[h][:, n * BANK : (n + 1) * BANK])
                 else:
+                    nc.scalar.copy(xw[h][:, n * BANK : (n + 1) * BANK], product[:])
                     nc.scalar.copy(sums[h][0][:, n * BANK : (n + 1) * BANK], product[:])
 
         a3 = [held.tile([P, S], BF16, name=f"a3_{h}") for h in range(h_blocks)]
+        result = held.tile([P, S], F32, name="result")
         begin = 0
         for width in PIECES:
             end = begin + width
@@ -191,7 +199,6 @@ def tile_gcnclassifer_b_kernel(
                         y_chunk[:, 0 : hi - lo], w4[:, h, :], a3[h][:, lo:hi], start=(h == 0), stop=(h == h_blocks - 1)
                     )
             for (lo, hi), y_chunk in zip(chunks, y):
-                result = results.tile([P, BANK], F32, name="result")
-                nc.scalar.copy(result[:, 0 : hi - lo], y_chunk[:, 0 : hi - lo])
-                nc.sync.dma_start(out[:, lo:hi], result[:, 0 : hi - lo])
+                nc.scalar.copy(result[:, lo:hi], y_chunk[:, 0 : hi - lo])
+                nc.sync.dma_start(out[:, lo:hi], result[:, lo:hi])
             begin = end

@@ -87,21 +87,21 @@ def tile_gcnclassifer_b_kernel(
         for i in range(WARM_UP):
             nc.tensor.matmul(unread[:], zeros[:, 0:P], zeros[:], start=True, stop=True)
 
+        minus_half = held.tile([P, d_blocks], F32, name="minus_half")
+        nc.gpsimd.memset(minus_half[:], -0.5)
         lin_b1 = load_column(nc, held, enc_b1, "lin_b1")
         gain1 = load_column(nc, held, bn1_gain, "gain1")
         shift1 = load_column(nc, held, bn1_shift, "shift1")
         mean1 = load_column(nc, held, bn1_mean, "mean1")
         var1 = load_column(nc, held, bn1_var, "var1")
+        scale1, bias1 = fold_batch_norm(nc, held, 1, lin_b1, gain1, shift1, mean1, var1, minus_half)
         lin_b2 = load_column(nc, held, enc_b2, "lin_b2")
         gain2 = load_column(nc, held, bn2_gain, "gain2")
         shift2 = load_column(nc, held, bn2_shift, "shift2")
         mean2 = load_column(nc, held, bn2_mean, "mean2")
         var2 = load_column(nc, held, bn2_var, "var2")
-        bias3 = load_column(nc, held, gcn1_b, "bias3")
-        minus_half = held.tile([P, d_blocks], F32, name="minus_half")
-        nc.gpsimd.memset(minus_half[:], -0.5)
-        scale1, bias1 = fold_batch_norm(nc, held, 1, lin_b1, gain1, shift1, mean1, var1, minus_half)
         scale2, bias2 = fold_batch_norm(nc, held, 2, lin_b2, gain2, shift2, mean2, var2, minus_half)
+        bias3 = load_column(nc, held, gcn1_b, "bias3")
 
         w1 = [held.tile([P, D1], BF16, name=f"w1_{k}") for k in range(f_blocks)]
         for k in range(f_blocks):

@@ -173,32 +173,46 @@ def tile_gcnclassifer_b_kernel(
 
         a3 = [held.tile([P, S], BF16, name=f"a3_{h}") for h in range(h_blocks)]
         result = held.tile([P, S], F32, name="result")
-        begin = 0
-        for width in PIECES:
-            end = begin + width
-            chunks = [(lo, min(lo + BANK, end)) for lo in range(begin, end, BANK)]
-            y = [psum.tile([P, BANK], F32, name=f"y_{lo}", tag="bank") for lo, hi in chunks]
-            for h in range(h_blocks):
-                for r in range(ROUNDS):
-                    first = (r * S + begin) // 16
-                    nc.vector.tensor_tensor(
-                        out=sums[h][(r + 1) % 2][:, begin:end],
-                        in0=xw[h][:].indirect(offsets[:, first : first + width // 16]),
-                        in1=sums[h][r % 2][:, begin:end],
-                        op=ADD,
-                    )
-                for (lo, hi), y_chunk in zip(chunks, y):
-                    nc.scalar.activation(
-                        a3[h][:, lo:hi],
-                        sums[h][ROUNDS % 2][:, lo:hi],
-                        RELU,
-                        bias=bias3[:, h : h + 1],
-                        scale=1.0 / (ROUNDS + 1),
-                    )
-                    nc.tensor.matmul(
-                        y_chunk[:, 0 : hi - lo], w4[:, h, :], a3[h][:, lo:hi], start=(h == 0), stop=(h == h_blocks - 1)
-                    )
-            for (lo, hi), y_chunk in zip(chunks, y):
-                nc.scalar.copy(result[:, lo:hi], y_chunk[:, 0 : hi - lo])
+
+        def look_up_and_add(h, r, begin, end):
+            first = (r * S + begin) // 16
+            nc.vector.tensor_tensor(
+                out=sums[h][(r + 1) % 2][:, begin:end],
+                in0=xw[h][:].indirect(offsets[:, first : first + (end - begin) // 16]),
+                in1=sums[h][r % 2][:, begin:end],
+                op=ADD,
+            )
+
+        def relu_and_multiply(h, lo, hi, y_chunk):
+            nc.scalar.activation(
+                a3[h][:, lo:hi],
+                sums[h][ROUNDS % 2][:, lo:hi],
+                RELU,
+                bias=bias3[:, h : h + 1],
+                scale=1.0 / (ROUNDS + 1),
+            )
+            nc.tensor.matmul(
+                y_chunk[:, 0 : hi - lo], w4[:, h, :], a3[h][:, lo:hi], start=(h == 0), stop=(h == h_blocks - 1)
+            )
+
+        ends = [sum(PIECES[: i + 1]) for i in range(len(PIECES))]
+        pieces = [(end - width, end) for width, end in zip(PIECES, ends)]
+        chunks = [[(lo, min(lo + BANK, end)) for lo in range(begin, end, BANK)] for begin, end in pieces]
+
+        for r in range(ROUNDS):
+            for half in range(2):
+                look_up_and_add(0, r, half * S // 2, (half + 1) * S // 2)
+        y = {}
+        for piece_chunks in chunks:
+            for lo, hi in piece_chunks:
+                y[lo] = psum.tile([P, BANK], F32, name=f"y_{lo}", tag="bank")
+                relu_and_multiply(0, lo, hi, y[lo])
+
+        for (begin, end), piece_chunks in zip(pieces, chunks):
+            for r in range(ROUNDS):
+                look_up_and_add(1, r, begin, end)
+            for lo, hi in piece_chunks:
+                relu_and_multiply(1, lo, hi, y[lo])
+            for lo, hi in piece_chunks:
+                nc.scalar.copy(result[:, lo:hi], y[lo][:, 0 : hi - lo])
                 nc.sync.dma_start(out[:, lo:hi], result[:, lo:hi])
-            begin = end

@@ -16,7 +16,7 @@ ROUNDS = 2
 BN_EPS = 1e-5
 BANK = 512
 WARM_UP = 5
-PIECES = (1024, 512, 256, 256)
+PIECES = (1024, 512, 256, 128, 128)
 assert sum(PIECES) == S
 
 FLOPS = 2 * S * (F * D1 + D1 * E + E * H + H * Q)
@@ -208,11 +208,14 @@ def tile_gcnclassifer_b_kernel(
                 y[lo] = psum.tile([P, BANK], F32, name=f"y_{lo}", tag="bank")
                 relu_and_multiply(0, lo, hi, y[lo])
 
-        for (begin, end), piece_chunks in zip(pieces, chunks):
+        stored = 0
+        for i, ((begin, end), piece_chunks) in enumerate(zip(pieces, chunks)):
             for r in range(ROUNDS):
                 look_up_and_add(1, r, begin, end)
             for lo, hi in piece_chunks:
                 relu_and_multiply(1, lo, hi, y[lo])
             for lo, hi in piece_chunks:
                 nc.scalar.copy(result[:, lo:hi], y[lo][:, 0 : hi - lo])
-                nc.sync.dma_start(out[:, lo:hi], result[:, lo:hi])
+            if i != len(pieces) - 2:
+                nc.sync.dma_start(out[:, stored:end], result[:, stored:end])
+                stored = end

@@ -18,6 +18,8 @@ BANK = 512
 WARM_UP = 5
 PIECES = (1024, 512, 256, 128, 128)
 assert sum(PIECES) == S
+XW_PIECES = (BANK, BANK, BANK, BANK // 2, BANK // 2)
+assert sum(XW_PIECES) == S
 
 FLOPS = 2 * S * (F * D1 + D1 * E + E * H + H * Q)
 
@@ -154,22 +156,26 @@ def tile_gcnclassifer_b_kernel(
         xw = [held.tile([P, S], F32, name=f"xw_{h}") for h in range(h_blocks)]
         sums = [[held.tile([P, S], F32, name=f"sum_{h}_{i}") for i in range(2)] for h in range(h_blocks)]
         for h in range(h_blocks):
-            for n in range(banks):
+            for i, width in enumerate(XW_PIECES):
+                lo = sum(XW_PIECES[:i])
+                hi = lo + width
                 product = psum.tile([P, BANK], F32, name="product", tag="bank")
                 for k in range(e_blocks):
                     nc.tensor.matmul(
-                        product[:],
+                        product[:, 0:width],
                         columns_of_block(w3[:, k, :], h_blocks, h),
-                        a2[k][n][:],
+                        a2[k][lo // BANK][:, lo % BANK : lo % BANK + width],
                         start=(k == 0),
                         stop=(k == e_blocks - 1),
                     )
-                if h == 0:
-                    nc.vector.tensor_copy(xw[h][:, n * BANK : (n + 1) * BANK], product[:])
-                    nc.scalar.copy(sums[h][0][:, n * BANK : (n + 1) * BANK], xw[h][:, n * BANK : (n + 1) * BANK])
+                if h == 0 and i != 2:
+                    nc.vector.tensor_copy(xw[h][:, lo:hi], product[:, 0:width])
                 else:
-                    nc.scalar.copy(xw[h][:, n * BANK : (n + 1) * BANK], product[:])
-                    nc.scalar.copy(sums[h][0][:, n * BANK : (n + 1) * BANK], product[:])
+                    nc.scalar.copy(xw[h][:, lo:hi], product[:, 0:width])
+                if h == 0:
+                    nc.scalar.copy(sums[h][0][:, lo:hi], xw[h][:, lo:hi])
+                else:
+                    nc.scalar.copy(sums[h][0][:, lo:hi], product[:, 0:width])
 
         a3 = [held.tile([P, S], BF16, name=f"a3_{h}") for h in range(h_blocks)]
         result = held.tile([P, S], F32, name="result")
@@ -199,9 +205,10 @@ def tile_gcnclassifer_b_kernel(
         pieces = [(end - width, end) for width, end in zip(PIECES, ends)]
         chunks = [[(lo, min(lo + BANK, end)) for lo in range(begin, end, BANK)] for begin, end in pieces]
 
-        for r in range(ROUNDS):
-            for half in range(2):
-                look_up_and_add(0, r, half * S // 2, (half + 1) * S // 2)
+        for n in range(banks):
+            look_up_and_add(0, 0, n * BANK, (n + 1) * BANK)
+        for half in range(2):
+            look_up_and_add(0, 1, half * S // 2, (half + 1) * S // 2)
         y = {}
         for piece_chunks in chunks:
             for lo, hi in piece_chunks:

import concourse.mybir as mybir

F32 = mybir.dt.float32
BF16 = mybir.dt.bfloat16
U16 = mybir.dt.uint16
ADD = mybir.AluOpType.add
SUBTRACT = mybir.AluOpType.subtract
MULT = mybir.AluOpType.mult
POW = mybir.AluOpType.pow
RELU = mybir.ActivationFunctionType.Relu

P = 128
F, D1, E, H, Q = 1024, 512, 256, 256, 128
S = 2048
ROUNDS = 2
BN_EPS = 1e-5
BANK = 512
WARM_UP = 5
PIECES = (1024, 512, 256, 128, 128)
assert sum(PIECES) == S
XW_PIECES = (BANK, BANK, BANK, BANK // 2, BANK // 2)
assert sum(XW_PIECES) == S

FLOPS = 2 * S * (F * D1 + D1 * E + E * H + H * Q)


def rows_in_blocks(matrix, blocks):
    return matrix.rearrange("(p c) n -> p c n", c=blocks)


def columns_of_block(weights, blocks, c):
    return weights.rearrange("p (j c) -> p c j", c=blocks)[:, c, :]


def load_column(nc, pool, column, name):
    blocks = column.shape[0] // P
    tile = pool.tile([P, blocks], F32, name=name)
    nc.gpsimd.dma_start(tile[:], column.rearrange("(p c) one -> p (c one)", c=blocks))
    return tile


def fold_batch_norm(nc, pool, layer, lin_bias, gain, shift, mean, var, minus_half):
    blocks = var.shape[1]
    scale = pool.tile([P, blocks], F32, name=f"scale{layer}")
    bias = pool.tile([P, blocks], F32, name=f"bias{layer}")
    nc.gpsimd.tensor_scalar(out=scale[:], in0=var[:], scalar1=BN_EPS, scalar2=None, op0=ADD)
    nc.gpsimd.tensor_tensor(out=scale[:], in0=scale[:], in1=minus_half[:, 0:blocks], op=POW)
    nc.gpsimd.tensor_tensor(out=scale[:], in0=scale[:], in1=gain[:], op=MULT)
    nc.gpsimd.tensor_tensor(out=bias[:], in0=lin_bias[:], in1=mean[:], op=SUBTRACT)
    nc.gpsimd.tensor_tensor(out=bias[:], in0=bias[:], in1=scale[:], op=MULT)
    nc.gpsimd.tensor_tensor(out=bias[:], in0=bias[:], in1=shift[:], op=ADD)
    return scale, bias


def tile_gcnclassifer_b_kernel(
    tc,
    feature,
    enc_w1,
    enc_b1,
    bn1_gain,
    bn1_shift,
    bn1_mean,
    bn1_var,
    enc_w2,
    enc_b2,
    bn2_gain,
    bn2_shift,
    bn2_mean,
    bn2_var,
    gcn1_w,
    gcn1_b,
    gcn2_w,
    offs,
    out,
):
    nc = tc.nc
    f_blocks, d_blocks, e_blocks, h_blocks = F // P, D1 // P, E // P, H // P
    banks = S // BANK

    with (
        tc.tile_pool(name="held", bufs=1) as held,
        tc.tile_pool(name="staged", bufs=8) as staged,
        tc.tile_pool(name="rounded", bufs=16) as rounded,
        tc.psum_pool(name="psum", bufs=8) as psum,
    ):
        zeros = held.tile([P, BANK], BF16, name="zeros")
        nc.vector.memset(zeros[:], 0.0)
        unread = psum.tile([P, BANK], F32, name="unread", tag="bank")
        for i in range(WARM_UP):
            nc.tensor.matmul(unread[:], zeros[:, 0:P], zeros[:], start=True, stop=True)

        minus_half = held.tile([P, d_blocks], F32, name="minus_half")
        nc.gpsimd.memset(minus_half[:], -0.5)
        lin_b1 = load_column(nc, held, enc_b1, "lin_b1")
        gain1 = load_column(nc, held, bn1_gain, "gain1")
        shift1 = load_column(nc, held, bn1_shift, "shift1")
        mean1 = load_column(nc, held, bn1_mean, "mean1")
        var1 = load_column(nc, held, bn1_var, "var1")
        scale1, bias1 = fold_batch_norm(nc, held, 1, lin_b1, gain1, shift1, mean1, var1, minus_half)
        lin_b2 = load_column(nc, held, enc_b2, "lin_b2")
        gain2 = load_column(nc, held, bn2_gain, "gain2")
        shift2 = load_column(nc, held, bn2_shift, "shift2")
        mean2 = load_column(nc, held, bn2_mean, "mean2")
        var2 = load_column(nc, held, bn2_var, "var2")
        scale2, bias2 = fold_batch_norm(nc, held, 2, lin_b2, gain2, shift2, mean2, var2, minus_half)
        bias3 = load_column(nc, held, gcn1_b, "bias3")

        w1 = [held.tile([P, D1], BF16, name=f"w1_{k}") for k in range(f_blocks)]
        for k in range(f_blocks):
            nc.scalar.dma_start(w1[k][:], rows_in_blocks(enc_w1, f_blocks)[:, k, :])
        w2 = held.tile([P, d_blocks, E], BF16, name="w2")
        nc.scalar.dma_start(w2[:], rows_in_blocks(enc_w2, d_blocks))
        w3 = held.tile([P, e_blocks, H], BF16, name="w3")
        nc.scalar.dma_start(w3[:], rows_in_blocks(gcn1_w, e_blocks))
        w4 = held.tile([P, h_blocks, Q], BF16, name="w4")
        nc.scalar.dma_start(w4[:], rows_in_blocks(gcn2_w, h_blocks))

        a1 = [[held.tile([P, BANK], BF16, name=f"a1_{m}_{n}") for n in range(banks)] for m in range(d_blocks)]
        for n in range(banks):
            z1 = [psum.tile([P, BANK], F32, name=f"z1_{m}", tag="bank") for m in range(d_blocks)]
            for k in range(f_blocks):
                loaded = staged.tile([P, BANK], F32, name="loaded")
                nc.sync.dma_start(loaded[:], rows_in_blocks(feature, f_blocks)[:, k, n * BANK : (n + 1) * BANK])
                x = rounded.tile([P, BANK], BF16, name="x")
                nc.vector.tensor_copy(x[:], loaded[:])
                for m in range(d_blocks):
                    nc.tensor.matmul(
                        z1[m][:],
                        columns_of_block(w1[k][:], d_blocks, m),
                        x[:],
                        start=(k == 0),
                        stop=(k == f_blocks - 1),
                    )
            for m in range(d_blocks):
                nc.scalar.activation(
                    a1[m][n][:], z1[m][:], RELU, bias=bias1[:, m : m + 1], scale=scale1[:, m : m + 1]
                )

        offsets = held.tile([P, ROUNDS * S // 16], U16, name="offsets")
        nc.sync.dma_start(offsets[:], offs)

        a2 = [[held.tile([P, BANK], BF16, name=f"a2_{m}_{n}") for n in range(banks)] for m in range(e_blocks)]
        for n in range(banks):
            for m in range(e_blocks):
                z2 = psum.tile([P, BANK], F32, name="z2", tag="bank")
                for k in range(d_blocks):
                    nc.tensor.matmul(
                        z2[:],
                        columns_of_block(w2[:, k, :], e_blocks, m),
                        a1[k][n][:],
                        start=(k == 0),
                        stop=(k == d_blocks - 1),
                    )
                nc.scalar.activation(a2[m][n][:], z2[:], RELU, bias=bias2[:, m : m + 1], scale=scale2[:, m : m + 1])

        xw = [held.tile([P, S], F32, name=f"xw_{h}") for h in range(h_blocks)]
        sums = [[held.tile([P, S], F32, name=f"sum_{h}_{i}") for i in range(2)] for h in range(h_blocks)]
        for h in range(h_blocks):
            for i, width in enumerate(XW_PIECES):
                lo = sum(XW_PIECES[:i])
                hi = lo + width
                product = psum.tile([P, BANK], F32, name="product", tag="bank")
                for k in range(e_blocks):
                    nc.tensor.matmul(
                        product[:, 0:width],
                        columns_of_block(w3[:, k, :], h_blocks, h),
                        a2[k][lo // BANK][:, lo % BANK : lo % BANK + width],
                        start=(k == 0),
                        stop=(k == e_blocks - 1),
                    )
                if h == 0 and i != 2:
                    nc.vector.tensor_copy(xw[h][:, lo:hi], product[:, 0:width])
                else:
                    nc.scalar.copy(xw[h][:, lo:hi], product[:, 0:width])
                if h == 0:
                    nc.scalar.copy(sums[h][0][:, lo:hi], xw[h][:, lo:hi])
                else:
                    nc.scalar.copy(sums[h][0][:, lo:hi], product[:, 0:width])

        a3 = [held.tile([P, S], BF16, name=f"a3_{h}") for h in range(h_blocks)]
        result = held.tile([P, S], F32, name="result")

        def look_up_and_add(h, r, begin, end):
            first = (r * S + begin) // 16
            nc.vector.tensor_tensor(
                out=sums[h][(r + 1) % 2][:, begin:end],
                in0=xw[h][:].indirect(offsets[:, first : first + (end - begin) // 16]),
                in1=sums[h][r % 2][:, begin:end],
                op=ADD,
            )

        def relu_and_multiply(h, lo, hi, y_chunk):
            nc.scalar.activation(
                a3[h][:, lo:hi],
                sums[h][ROUNDS % 2][:, lo:hi],
                RELU,
                bias=bias3[:, h : h + 1],
                scale=1.0 / (ROUNDS + 1),
            )
            nc.tensor.matmul(
                y_chunk[:, 0 : hi - lo], w4[:, h, :], a3[h][:, lo:hi], start=(h == 0), stop=(h == h_blocks - 1)
            )

        ends = [sum(PIECES[: i + 1]) for i in range(len(PIECES))]
        pieces = [(end - width, end) for width, end in zip(PIECES, ends)]
        chunks = [[(lo, min(lo + BANK, end)) for lo in range(begin, end, BANK)] for begin, end in pieces]

        for n in range(banks):
            look_up_and_add(0, 0, n * BANK, (n + 1) * BANK)
        for half in range(2):
            look_up_and_add(0, 1, half * S // 2, (half + 1) * S // 2)
        y = {}
        for piece_chunks in chunks:
            for lo, hi in piece_chunks:
                y[lo] = psum.tile([P, BANK], F32, name=f"y_{lo}", tag="bank")
                relu_and_multiply(0, lo, hi, y[lo])

        stored = 0
        for i, ((begin, end), piece_chunks) in enumerate(zip(pieces, chunks)):
            for r in range(ROUNDS):
                look_up_and_add(1, r, begin, end)
            for lo, hi in piece_chunks:
                relu_and_multiply(1, lo, hi, y[lo])
            for lo, hi in piece_chunks:
                nc.scalar.copy(result[:, lo:hi], y[lo][:, 0 : hi - lo])
            if i != len(pieces) - 2:
                nc.sync.dma_start(out[:, stored:end], result[:, stored:end])
                stored = end
